import numpy as np
import ml_dtypes


def mxq(x, axis, fmt="e4m3"):
    dtype, down = {"e4m3": (ml_dtypes.float8_e4m3fn, 7), "e5m2": (ml_dtypes.float8_e5m2, 14)}[fmt]
    v = np.moveaxis(np.asarray(x, np.float32).astype(ml_dtypes.bfloat16).astype(np.float64), axis, -1)
    blocks = v.reshape(v.shape[:-1] + (-1, 32))
    amax = np.abs(blocks).max(-1, keepdims=True)
    byte = np.maximum(np.where(amax > 0, np.frexp(amax)[1] - 1 + 127, 0) - down, 1)
    scale = np.exp2(byte - 127.0)
    codes = (blocks / scale).astype(np.float32).astype(dtype).astype(np.float64)
    return np.moveaxis((codes * scale).reshape(v.shape), -1, axis)


WIDE = False


def mx_kscale(k):
    if not WIDE:
        return np.ones(k)
    levels = np.array([10, -10, 5, -5, 0])
    a = np.random.permutation(np.resize(levels, k // 512 * 4)).reshape(k // 512, 4)
    idx = np.arange(k)
    return np.exp2(a[idx // 512, idx % 128 // 32])


BF16 = ml_dtypes.bfloat16


def bf(x):
    return np.asarray(x, np.float32).astype(BF16)


def f64(x):
    return np.asarray(x).astype(np.float64)


E2M1 = np.array([0.0, 0.5, 1.0, 1.5, 2.0, 3.0, 4.0, 6.0, -0.0, -0.5, -1.0, -1.5, -2.0, -3.0, -4.0, -6.0])


def pack_weight(w, fmt):
    k, n = w.shape
    w = f64(bf(w)).reshape(k // 32, 32, n)
    amax = np.abs(w).max(1)
    if fmt == "e4m3":
        byte = np.frexp(amax)[1] - 1 + 127 - 7
    else:
        mant, ex = np.frexp(amax / 6.0)
        byte = np.where(mant > 0.5, ex, ex - 1) + 127
    byte = np.clip(np.where(amax > 0, byte, 1), 1, 254)
    scaled = (w * np.exp2(127.0 - byte)[:, None, :]).reshape(k, n).astype(np.float32)
    by_word = np.ascontiguousarray(scaled.reshape(k // 512, 128, 4, n).transpose(0, 1, 3, 2))
    if fmt == "e4m3":
        words = by_word.astype(ml_dtypes.float8_e4m3fn).view(np.uint8)
    else:
        c = by_word.astype(ml_dtypes.float4_e2m1fn).view(np.uint8) & 0xF
        words = c[..., 0::2] | (c[..., 1::2] << 4)
    return np.ascontiguousarray(words), np.ascontiguousarray(byte.astype(np.uint8).reshape(k // 512, 16, n))


def unpack_weight(words, scales, fmt):
    g, p, n, _ = words.shape
    if fmt == "e4m3":
        vals = np.ascontiguousarray(words).view(ml_dtypes.float8_e4m3fn).astype(np.float64)
    else:
        nib = np.empty((g, p, n, 4), np.uint8)
        nib[..., 0::2] = words & 0xF
        nib[..., 1::2] = words >> 4
        vals = E2M1[nib]
    vals = vals * np.repeat(np.exp2(scales.astype(np.float64) - 127.0), 8, axis=1)[..., None]
    return vals.transpose(0, 1, 3, 2).reshape(g * 512, n)


B, N, D = 1, 1024, 1024
P0 = 0.2
FMT = "e4m3"


def setup_inputs():
    s = mx_kscale(D)
    g = 0.4 + 1.2 * np.random.random_sample((B, 1, N))
    bound = np.sqrt(6.0 / (D + D))
    embedding = bf(np.random.standard_normal((B, D, N)) * g * np.sqrt(P0) / D ** 0.25 * s[None, :, None])
    heatm = bf(np.random.standard_normal((B, D, N)))
    words, scales = pack_weight(np.random.uniform(-bound, bound, (D, D)) / s[:, None] / s[None, :], FMT)
    return {"embedding": embedding,
            "heatm": heatm,
            "W_b_words": words,
            "W_b_scales": scales}


def reference(embedding, heatm, W_b_words, W_b_scales):
    eq = mxq(f64(embedding), 1, "e4m3")
    t = np.swapaxes(eq, 1, 2) @ unpack_weight(W_b_words, W_b_scales, FMT)
    C = np.tanh(mxq(t, 2, "e4m3") @ eq)
    max_cow = np.max(C, axis=-1, keepdims=True)
    e = np.exp(max_cow - np.max(max_cow, axis=1, keepdims=True))
    return e / np.sum(e, axis=1, keepdims=True)

@@ -1,0 +1,216 @@
+from contextlib import ExitStack
+
+import concourse.mybir as mybir
+from concourse.masks import make_identity
+
+F32 = mybir.dt.float32
+BF16 = mybir.dt.bfloat16
+I32 = mybir.dt.int32
+U32 = mybir.dt.uint32
+U8 = mybir.dt.uint8
+FP8X4 = mybir.dt.float8_e4m3fn_x4
+ACT = mybir.ActivationFunctionType
+ALU = mybir.AluOpType
+AXIS_X = mybir.AxisListType.X
+
+P = 128
+PACK = 4
+K_PASS = P * PACK
+D = 1024
+N = 1024
+PASSES = D // K_PASS
+BANK = 512
+HALVES = N // BANK
+ROW_TILES = N // P
+RUN = 4
+TURN_LAG = 1
+SECOND_LAG = 3
+
+FLOPS = 2 * 2 * N * D * N
+BYTES = 2 * D * N + D * D + D * D // 32 + 4 * N
+
+
+def tile_parallelcoattention_kernel(tc, embedding, heatm, W_b_words, W_b_scales, out):
+    nc = tc.nc
+    with ExitStack() as ctx:
+        keep = ctx.enter_context(tc.tile_pool(name="keep", bufs=1))
+        sorted_pool = ctx.enter_context(tc.tile_pool(name="sorted", bufs=3))
+        grouped_pool = ctx.enter_context(tc.tile_pool(name="grouped", bufs=2))
+        quantised_pool = ctx.enter_context(tc.tile_pool(name="quantised", bufs=SECOND_LAG + 1))
+        first_psum = ctx.enter_context(tc.psum_pool(name="first_psum", bufs=3))
+        turned_psum = ctx.enter_context(tc.psum_pool(name="turned_psum", bufs=2))
+        second_psum = ctx.enter_context(tc.psum_pool(name="second_psum", bufs=3))
+
+        e_raw = keep.tile([P, PASSES, PACK, N], BF16)
+        e_grouped = keep.tile([P, PASSES, N, PACK], BF16, align_bytes=64)
+        e_codes = keep.tile([P, PASSES, N], U32, align_bytes=64)
+        e_scales = keep.tile([P, PASSES, N], U8, align_bytes=64)
+        w_codes = keep.tile([P, PASSES, D], U32, align_bytes=64)
+        w_scales = keep.tile([P, PASSES, D], U8, align_bytes=64)
+        ident_bf16 = keep.tile([P, P], BF16)
+        ident_f32 = keep.tile([P, P], F32)
+        half_max = keep.tile([P, ROW_TILES * HALVES], F32)
+        exp_padded = keep.tile([P, P], F32)
+        table_warm = keep.tile([P, 1], F32)
+
+        nc.vector.memset(w_scales[:].bitcast(I32), 0)
+        nc.vector.memset(exp_padded[:], 0.0)
+        nc.vector.memset(table_warm[:], 0.0)
+        nc.scalar.activation(out=table_warm[:], in_=table_warm[:], func=ACT.Tanh)
+        make_identity(nc, ident_bf16[:])
+        make_identity(nc, ident_f32[:])
+
+        def load_embedding_half(half):
+            cols = slice(half * BANK, (half + 1) * BANK)
+            for g in range(PASSES):
+                rows = embedding[0, g * K_PASS : (g + 1) * K_PASS, cols]
+                nc.sync.dma_start(
+                    out=e_raw[:, g, :, cols], in_=rows.rearrange("(p j) n -> p j n", j=PACK)
+                )
+
+        load_embedding_half(0)
+        for r in range(4):
+            nc.sync.dma_start(
+                out=w_scales[r:P:32, :, :].bitcast(I32),
+                in_=W_b_scales[:, r:16:4, :].rearrange("g q n -> q g n").bitcast(I32),
+            )
+        for g in range(PASSES):
+            nc.sync.dma_start(
+                out=w_codes[:, g, :].bitcast(I32),
+                in_=W_b_words[g].rearrange("p n j -> p (n j)").bitcast(I32),
+            )
+        load_embedding_half(1)
+
+        def regroup(copy, g, cols):
+            copy(
+                out=e_grouped[:, g, cols, :].rearrange("p (c i) j -> p c j i", i=RUN),
+                in_=e_raw[:, g, :, cols].rearrange("p j (c i) -> p c j i", i=RUN),
+            )
+
+        def quantise_embedding(g, cols):
+            nc.vector.quantize_mx(
+                out=e_codes[:, g, cols].bitcast(FP8X4),
+                scales=e_scales[:, g, cols],
+                in_=e_grouped[:, g, cols, :].rearrange("p n j -> p (n j)"),
+            )
+
+        middle = BANK // 2
+        for g in range(PASSES):
+            regroup(nc.vector.tensor_copy, g, slice(0, middle))
+            regroup(nc.scalar.copy, g, slice(middle, BANK))
+        for g in range(PASSES):
+            quantise_embedding(g, slice(0, BANK))
+        for g in range(PASSES):
+            regroup(nc.vector.tensor_copy, g, slice(BANK, N))
+        for g in range(PASSES):
+            quantise_embedding(g, slice(BANK, N))
+
+        t_sorted = {}
+        t_codes = {}
+        t_scales = {}
+
+        def first_product(i):
+            rows = slice(i * P, (i + 1) * P)
+            t_sorted[i] = sorted_pool.tile([P, PASSES, PACK, P], BF16, name="t_sorted")
+            for g2 in range(PASSES):
+                cols = slice(g2 * BANK, (g2 + 1) * BANK)
+                t_sum = first_psum.tile([P, BANK], F32, name="t_sum", tag="first")
+                for g in range(PASSES):
+                    nc.tensor.matmul_mx(
+                        out=t_sum[:],
+                        lhsT=e_codes[:, g, rows].bitcast(FP8X4),
+                        lhsT_scale=e_scales[:, g, rows],
+                        rhs=w_codes[:, g, cols].bitcast(FP8X4),
+                        rhs_scale=w_scales[:, g, cols],
+                        start=(g == 0),
+                        stop=(g == PASSES - 1),
+                    )
+                nc.scalar.copy(
+                    out=t_sorted[i][:, g2, :, :],
+                    in_=t_sum[:].rearrange("n (p j) -> n j p", j=PACK),
+                )
+
+        def turn_and_quantise(i):
+            turned = turned_psum.tile([P, PASSES, PACK, P], BF16, name="turned")
+            for g2 in range(PASSES):
+                for j in range(PACK):
+                    nc.tensor.transpose(turned[:, g2, j, :], t_sorted[i][:, g2, j, :], ident_bf16[:])
+            t_grouped = grouped_pool.tile([P, PASSES, P, PACK], BF16, name="t_grouped", align_bytes=64)
+            nc.scalar.copy(out=t_grouped[:], in_=turned[:].rearrange("p g j n -> p g n j"))
+            t_codes[i] = quantised_pool.tile([P, PASSES, P], U32, name="t_codes", align_bytes=64)
+            t_scales[i] = quantised_pool.tile([P, PASSES, P], U8, name="t_scales", align_bytes=64)
+            nc.vector.quantize_mx(
+                out=t_codes[i][:].rearrange("p g n -> p (g n)").bitcast(FP8X4),
+                scales=t_scales[i][:].rearrange("p g n -> p (g n)"),
+                in_=t_grouped[:].rearrange("p g n j -> p (g n j)"),
+            )
+
+        def second_product(i):
+            for half in range(HALVES):
+                cols = slice(half * BANK, (half + 1) * BANK)
+                c_sum = second_psum.tile([P, BANK], F32, name="c_sum")
+                for g2 in range(PASSES):
+                    nc.tensor.matmul_mx(
+                        out=c_sum[:],
+                        lhsT=t_codes[i][:, g2, :].bitcast(FP8X4),
+                        lhsT_scale=t_scales[i][:, g2, :],
+                        rhs=e_codes[:, g2, cols].bitcast(FP8X4),
+                        rhs_scale=e_scales[:, g2, cols],
+                        start=(g2 == 0),
+                        stop=(g2 == PASSES - 1),
+                    )
+                place = i * HALVES + half
+                nc.vector.tensor_reduce(
+                    out=half_max[:, place : place + 1], in_=c_sum[:], axis=AXIS_X, op=ALU.max
+                )
+
+        for step in range(ROW_TILES + SECOND_LAG):
+            if step < ROW_TILES:
+                first_product(step)
+            if 0 <= step - SECOND_LAG:
+                second_product(step - SECOND_LAG)
+            if 0 <= step - TURN_LAG < ROW_TILES:
+                turn_and_quantise(step - TURN_LAG)
+
+        row_max = keep.tile([P, ROW_TILES], F32)
+        nc.vector.tensor_reduce(
+            out=row_max[:],
+            in_=half_max[:].rearrange("p (i h) -> p i h", h=HALVES),
+            axis=AXIS_X,
+            op=ALU.max,
+        )
+        m = keep.tile([P, ROW_TILES], F32)
+        nc.scalar.activation(out=m[:], in_=row_max[:], func=ACT.Tanh)
+
+        def over_all_partitions(column, op, name):
+            spread = first_psum.tile([P, P], F32, name=name + "_spread", tag="first")
+            nc.tensor.matmul(
+                out=spread[:],
+                lhsT=column[:, 0:1].to_broadcast([P, P]),
+                rhs=ident_f32[:],
+                start=True,
+                stop=True,
+            )
+            result = keep.tile([P, 1], F32, name=name)
+            nc.vector.tensor_reduce(out=result[:], in_=spread[:], axis=AXIS_X, op=op)
+            return result
+
+        partition_max = keep.tile([P, 1], F32)
+        nc.vector.tensor_reduce(out=partition_max[:], in_=m[:], axis=AXIS_X, op=ALU.max)
+        top = over_all_partitions(partition_max, ALU.max, "top")
+        shifted = keep.tile([P, ROW_TILES], F32)
+        nc.vector.tensor_scalar_sub(out=shifted[:], in0=m[:], scalar1=top[:, 0:1])
+        partition_sum = keep.tile([P, 1], F32)
+        nc.scalar.activation(
+            out=exp_padded[:, 0:ROW_TILES], in_=shifted[:], func=ACT.Exp, accum_out=partition_sum[:]
+        )
+        total = over_all_partitions(partition_sum, ALU.add, "total")
+        inverse = keep.tile([P, 1], F32)
+        nc.vector.reciprocal(out=inverse[:], in_=total[:])
+        exp_turned = first_psum.tile([P, P], F32, name="exp_turned", tag="first")
+        nc.tensor.transpose(exp_turned[:], exp_padded[:], ident_f32[:])
+        weights = keep.tile([P, P], F32)
+        nc.vector.tensor_scalar_mul(out=weights[:], in0=exp_turned[:], scalar1=inverse[:, 0:1])
+        nc.sync.dma_start(
+            out=out[0].rearrange("(i p) o -> i (p o)", p=P), in_=weights[0:ROW_TILES, :]
+        )

@@ -23,8 +23,10 @@ BANK = 512
 HALVES = N // BANK
 ROW_TILES = N // P
 RUN = 4
-TURN_LAG = 1
-SECOND_LAG = 3
+STEP_TILES = 2
+STEPS = ROW_TILES // STEP_TILES
+STEP_COLS = STEP_TILES * P
+SUM_BANKS = 6
 
 FLOPS = 2 * 2 * N * D * N
 BYTES = 2 * D * N + D * D + D * D // 32 + 4 * N
@@ -33,13 +35,13 @@ BYTES = 2 * D * N + D * D + D * D // 32 + 4 * N
 def tile_parallelcoattention_kernel(tc, embedding, heatm, W_b_words, W_b_scales, out):
     nc = tc.nc
     with ExitStack() as ctx:
+        ctx.enter_context(tc.manual_schedule())
         keep = ctx.enter_context(tc.tile_pool(name="keep", bufs=1))
-        sorted_pool = ctx.enter_context(tc.tile_pool(name="sorted", bufs=3))
-        grouped_pool = ctx.enter_context(tc.tile_pool(name="grouped", bufs=2))
-        quantised_pool = ctx.enter_context(tc.tile_pool(name="quantised", bufs=SECOND_LAG + 1))
-        first_psum = ctx.enter_context(tc.psum_pool(name="first_psum", bufs=3))
-        turned_psum = ctx.enter_context(tc.psum_pool(name="turned_psum", bufs=2))
-        second_psum = ctx.enter_context(tc.psum_pool(name="second_psum", bufs=3))
+        sorted_pool = ctx.enter_context(tc.tile_pool(name="sorted", bufs=2 * STEP_TILES))
+        grouped_pool = ctx.enter_context(tc.tile_pool(name="grouped", bufs=2 * STEP_TILES))
+        quantised_pool = ctx.enter_context(tc.tile_pool(name="quantised", bufs=2 * STEP_TILES))
+        sum_psum = ctx.enter_context(tc.psum_pool(name="sum_psum", bufs=SUM_BANKS))
+        turned_psum = ctx.enter_context(tc.psum_pool(name="turned_psum", bufs=STEP_TILES))
 
         e_raw = keep.tile([P, PASSES, PACK, N], BF16)
         e_grouped = keep.tile([P, PASSES, N, PACK], BF16, align_bytes=64)
@@ -60,50 +62,42 @@ def tile_parallelcoattention_kernel(tc, embedding, heatm, W_b_words, W_b_scales,
         make_identity(nc, ident_bf16[:])
         make_identity(nc, ident_f32[:])
 
-        def load_embedding_half(half):
-            cols = slice(half * BANK, (half + 1) * BANK)
+        def load_embedding(step):
+            cols = slice(step * STEP_COLS, (step + 1) * STEP_COLS)
             for g in range(PASSES):
                 rows = embedding[0, g * K_PASS : (g + 1) * K_PASS, cols]
                 nc.sync.dma_start(
                     out=e_raw[:, g, :, cols], in_=rows.rearrange("(p j) n -> p j n", j=PACK)
                 )
 
-        load_embedding_half(0)
+        load_embedding(0)
         for r in range(4):
             nc.sync.dma_start(
                 out=w_scales[r:P:32, :, :].bitcast(I32),
                 in_=W_b_scales[:, r:16:4, :].rearrange("g q n -> q g n").bitcast(I32),
             )
-        for g in range(PASSES):
+        for half in range(HALVES):
+            cols = slice(half * BANK, (half + 1) * BANK)
             nc.sync.dma_start(
-                out=w_codes[:, g, :].bitcast(I32),
-                in_=W_b_words[g].rearrange("p n j -> p (n j)").bitcast(I32),
+                out=w_codes[:, :, cols].bitcast(I32),
+                in_=W_b_words[:, :, cols, :].rearrange("g p n j -> p g (n j)").bitcast(I32),
             )
-        load_embedding_half(1)
+        for step in range(1, STEPS):
+            load_embedding(step)
 
-        def regroup(copy, g, cols):
-            copy(
-                out=e_grouped[:, g, cols, :].rearrange("p (c i) j -> p c j i", i=RUN),
-                in_=e_raw[:, g, :, cols].rearrange("p j (c i) -> p c j i", i=RUN),
-            )
-
-        def quantise_embedding(g, cols):
-            nc.vector.quantize_mx(
-                out=e_codes[:, g, cols].bitcast(FP8X4),
-                scales=e_scales[:, g, cols],
-                in_=e_grouped[:, g, cols, :].rearrange("p n j -> p (n j)"),
-            )
-
-        middle = BANK // 2
-        for g in range(PASSES):
-            regroup(nc.vector.tensor_copy, g, slice(0, middle))
-            regroup(nc.scalar.copy, g, slice(middle, BANK))
-        for g in range(PASSES):
-            quantise_embedding(g, slice(0, BANK))
-        for g in range(PASSES):
-            regroup(nc.vector.tensor_copy, g, slice(BANK, N))
-        for g in range(PASSES):
-            quantise_embedding(g, slice(BANK, N))
+        for step in range(STEPS):
+            cols = slice(step * STEP_COLS, (step + 1) * STEP_COLS)
+            for g in range(PASSES):
+                nc.vector.tensor_copy(
+                    out=e_grouped[:, g, cols, :].rearrange("p (c i) j -> p c j i", i=RUN),
+                    in_=e_raw[:, g, :, cols].rearrange("p j (c i) -> p c j i", i=RUN),
+                )
+            for g in range(PASSES):
+                nc.vector.quantize_mx(
+                    out=e_codes[:, g, cols].bitcast(FP8X4),
+                    scales=e_scales[:, g, cols],
+                    in_=e_grouped[:, g, cols, :].rearrange("p n j -> p (n j)"),
+                )
 
         t_sorted = {}
         t_codes = {}
@@ -114,7 +108,7 @@ def tile_parallelcoattention_kernel(tc, embedding, heatm, W_b_words, W_b_scales,
             t_sorted[i] = sorted_pool.tile([P, PASSES, PACK, P], BF16, name="t_sorted")
             for g2 in range(PASSES):
                 cols = slice(g2 * BANK, (g2 + 1) * BANK)
-                t_sum = first_psum.tile([P, BANK], F32, name="t_sum", tag="first")
+                t_sum = sum_psum.tile([P, BANK], F32, name="t_sum", tag="sum")
                 for g in range(PASSES):
                     nc.tensor.matmul_mx(
                         out=t_sum[:],
@@ -148,7 +142,7 @@ def tile_parallelcoattention_kernel(tc, embedding, heatm, W_b_words, W_b_scales,
         def second_product(i):
             for half in range(HALVES):
                 cols = slice(half * BANK, (half + 1) * BANK)
-                c_sum = second_psum.tile([P, BANK], F32, name="c_sum")
+                c_sum = sum_psum.tile([P, BANK], F32, name="c_sum", tag="sum")
                 for g2 in range(PASSES):
                     nc.tensor.matmul_mx(
                         out=c_sum[:],
@@ -164,13 +158,18 @@ def tile_parallelcoattention_kernel(tc, embedding, heatm, W_b_words, W_b_scales,
                     out=half_max[:, place : place + 1], in_=c_sum[:], axis=AXIS_X, op=ALU.max
                 )
 
-        for step in range(ROW_TILES + SECOND_LAG):
-            if step < ROW_TILES:
-                first_product(step)
-            if 0 <= step - SECOND_LAG:
-                second_product(step - SECOND_LAG)
-            if 0 <= step - TURN_LAG < ROW_TILES:
-                turn_and_quantise(step - TURN_LAG)
+        def tiles_of(step):
+            if 0 <= step < STEPS:
+                return range(step * STEP_TILES, (step + 1) * STEP_TILES)
+            return range(0)
+
+        for step in range(STEPS + 2):
+            for i in tiles_of(step):
+                first_product(i)
+            for i in tiles_of(step - 1):
+                turn_and_quantise(i)
+            for i in tiles_of(step - 2):
+                second_product(i)
 
         row_max = keep.tile([P, ROW_TILES], F32)
         nc.vector.tensor_reduce(
@@ -183,7 +182,7 @@ def tile_parallelcoattention_kernel(tc, embedding, heatm, W_b_words, W_b_scales,
         nc.scalar.activation(out=m[:], in_=row_max[:], func=ACT.Tanh)
 
         def over_all_partitions(column, op, name):
-            spread = first_psum.tile([P, P], F32, name=name + "_spread", tag="first")
+            spread = sum_psum.tile([P, P], F32, name=name + "_spread", tag="sum")
             nc.tensor.matmul(
                 out=spread[:],
                 lhsT=column[:, 0:1].to_broadcast([P, P]),
@@ -204,11 +203,11 @@ def tile_parallelcoattention_kernel(tc, embedding, heatm, W_b_words, W_b_scales,
         nc.scalar.activation(
             out=exp_padded[:, 0:ROW_TILES], in_=shifted[:], func=ACT.Exp, accum_out=partition_sum[:]
         )
+        exp_turned = sum_psum.tile([P, P], F32, name="exp_turned", tag="sum")
+        nc.tensor.transpose(exp_turned[:], exp_padded[:], ident_f32[:])
         total = over_all_partitions(partition_sum, ALU.add, "total")
         inverse = keep.tile([P, 1], F32)
         nc.vector.reciprocal(out=inverse[:], in_=total[:])
-        exp_turned = first_psum.tile([P, P], F32, name="exp_turned", tag="first")
-        nc.tensor.transpose(exp_turned[:], exp_padded[:], ident_f32[:])
         weights = keep.tile([P, P], F32)
         nc.vector.tensor_scalar_mul(out=weights[:], in0=exp_turned[:], scalar1=inverse[:, 0:1])
         nc.sync.dma_start(

@@ -53,11 +53,13 @@ def tile_parallelcoattention_kernel(tc, embedding, heatm, W_b_words, W_b_scales,
         ident_f32 = keep.tile([P, P], F32)
         half_max = keep.tile([P, ROW_TILES * HALVES], F32)
         exp_padded = keep.tile([P, P], F32)
+        ones = keep.tile([P, P], F32)
         table_warm = keep.tile([P, 1], F32)
 
         nc.vector.memset(w_scales[:].bitcast(I32), 0)
         nc.vector.memset(exp_padded[:], 0.0)
         nc.vector.memset(table_warm[:], 0.0)
+        nc.vector.memset(ones[:], 1.0)
         nc.scalar.activation(out=table_warm[:], in_=table_warm[:], func=ACT.Tanh)
         make_identity(nc, ident_bf16[:])
         make_identity(nc, ident_f32[:])
@@ -171,6 +173,10 @@ def tile_parallelcoattention_kernel(tc, embedding, heatm, W_b_words, W_b_scales,
             for i in tiles_of(step - 2):
                 second_product(i)
 
+        partition_max = keep.tile([P, 1], F32)
+        nc.vector.tensor_reduce(out=partition_max[:], in_=half_max[:], axis=AXIS_X, op=ALU.max)
+        max_spread = sum_psum.tile([P, P], F32, name="max_spread", tag="sum")
+        nc.tensor.transpose(max_spread[:], partition_max[:, 0:1].to_broadcast([P, P]), ident_f32[:])
         row_max = keep.tile([P, ROW_TILES], F32)
         nc.vector.tensor_reduce(
             out=row_max[:],
@@ -180,32 +186,22 @@ def tile_parallelcoattention_kernel(tc, embedding, heatm, W_b_words, W_b_scales,
         )
         m = keep.tile([P, ROW_TILES], F32)
         nc.scalar.activation(out=m[:], in_=row_max[:], func=ACT.Tanh)
-
-        def over_all_partitions(column, op, name):
-            spread = sum_psum.tile([P, P], F32, name=name + "_spread", tag="sum")
-            nc.tensor.matmul(
-                out=spread[:],
-                lhsT=column[:, 0:1].to_broadcast([P, P]),
-                rhs=ident_f32[:],
-                start=True,
-                stop=True,
-            )
-            result = keep.tile([P, 1], F32, name=name)
-            nc.vector.tensor_reduce(out=result[:], in_=spread[:], axis=AXIS_X, op=op)
-            return result
-
-        partition_max = keep.tile([P, 1], F32)
-        nc.vector.tensor_reduce(out=partition_max[:], in_=m[:], axis=AXIS_X, op=ALU.max)
-        top = over_all_partitions(partition_max, ALU.max, "top")
-        shifted = keep.tile([P, ROW_TILES], F32)
-        nc.vector.tensor_scalar_sub(out=shifted[:], in0=m[:], scalar1=top[:, 0:1])
+        top_argument = keep.tile([P, 1], F32)
+        nc.vector.tensor_reduce(out=top_argument[:], in_=max_spread[:], axis=AXIS_X, op=ALU.max)
+        minus_top = keep.tile([P, 1], F32)
+        nc.scalar.activation(out=minus_top[:], in_=top_argument[:], func=ACT.Tanh, scale=-1.0)
         partition_sum = keep.tile([P, 1], F32)
         nc.scalar.activation(
-            out=exp_padded[:, 0:ROW_TILES], in_=shifted[:], func=ACT.Exp, accum_out=partition_sum[:]
+            out=exp_padded[:, 0:ROW_TILES],
+            in_=m[:],
+            func=ACT.Exp,
+            bias=minus_top[:, 0:1],
+            accum_out=partition_sum[:],
         )
         exp_turned = sum_psum.tile([P, P], F32, name="exp_turned", tag="sum")
         nc.tensor.transpose(exp_turned[:], exp_padded[:], ident_f32[:])
-        total = over_all_partitions(partition_sum, ALU.add, "total")
+        total = sum_psum.tile([P, 1], F32, name="total", tag="sum")
+        nc.tensor.matmul(out=total[:], lhsT=ones[:], rhs=partition_sum[:], start=True, stop=True)
         inverse = keep.tile([P, 1], F32)
         nc.vector.reciprocal(out=inverse[:], in_=total[:])
         weights = keep.tile([P, P], F32)

@@ -166,10 +166,10 @@ def tile_parallelcoattention_kernel(tc, embedding, heatm, W_b_words, W_b_scales,
             return range(0)
 
         for step in range(STEPS + 2):
-            for i in tiles_of(step):
-                first_product(i)
             for i in tiles_of(step - 1):
                 turn_and_quantise(i)
+            for i in tiles_of(step):
+                first_product(i)
             for i in tiles_of(step - 2):
                 second_product(i)
 

@@ -15,6 +15,8 @@ AXIS_X = mybir.AxisListType.X
 
 P = 128
 PACK = 4
+PAIR = 2
+PAIRS = PACK // PAIR
 K_PASS = P * PACK
 D = 1024
 N = 1024
@@ -49,7 +51,6 @@ def tile_parallelcoattention_kernel(tc, embedding, heatm, W_b_words, W_b_scales,
         e_scales = keep.tile([P, PASSES, N], U8, align_bytes=64)
         w_codes = keep.tile([P, PASSES, D], U32, align_bytes=64)
         w_scales = keep.tile([P, PASSES, D], U8, align_bytes=64)
-        ident_bf16 = keep.tile([P, P], BF16)
         ident_f32 = keep.tile([P, P], F32)
         half_max = keep.tile([P, ROW_TILES * HALVES], F32)
         exp_padded = keep.tile([P, P], F32)
@@ -61,7 +62,6 @@ def tile_parallelcoattention_kernel(tc, embedding, heatm, W_b_words, W_b_scales,
         nc.vector.memset(table_warm[:], 0.0)
         nc.vector.memset(ones[:], 1.0)
         nc.scalar.activation(out=table_warm[:], in_=table_warm[:], func=ACT.Tanh)
-        make_identity(nc, ident_bf16[:])
         make_identity(nc, ident_f32[:])
 
         def load_embedding(step):
@@ -107,7 +107,7 @@ def tile_parallelcoattention_kernel(tc, embedding, heatm, W_b_words, W_b_scales,
 
         def first_product(i):
             rows = slice(i * P, (i + 1) * P)
-            t_sorted[i] = sorted_pool.tile([P, PASSES, PACK, P], BF16, name="t_sorted")
+            t_sorted[i] = sorted_pool.tile([P, PASSES, PAIRS, P * PAIR], BF16, name="t_sorted")
             for g2 in range(PASSES):
                 cols = slice(g2 * BANK, (g2 + 1) * BANK)
                 t_sum = sum_psum.tile([P, BANK], F32, name="t_sum", tag="sum")
@@ -122,17 +122,23 @@ def tile_parallelcoattention_kernel(tc, embedding, heatm, W_b_words, W_b_scales,
                         stop=(g == PASSES - 1),
                     )
                 nc.scalar.copy(
-                    out=t_sorted[i][:, g2, :, :],
-                    in_=t_sum[:].rearrange("n (p j) -> n j p", j=PACK),
+                    out=t_sorted[i][:, g2, :, :].rearrange("n u (p e) -> n u p e", e=PAIR),
+                    in_=t_sum[:].rearrange("n (p u e) -> n u p e", u=PAIRS, e=PAIR),
                 )
 
         def turn_and_quantise(i):
-            turned = turned_psum.tile([P, PASSES, PACK, P], BF16, name="turned")
+            turned = turned_psum.tile([P, PASSES, PAIRS, P], F32, name="turned")
             for g2 in range(PASSES):
-                for j in range(PACK):
-                    nc.tensor.transpose(turned[:, g2, j, :], t_sorted[i][:, g2, j, :], ident_bf16[:])
+                for u in range(PAIRS):
+                    nc.tensor.transpose(
+                        turned[:, g2, u, :], t_sorted[i][:, g2, u, :].bitcast(F32), ident_f32[:]
+                    )
             t_grouped = grouped_pool.tile([P, PASSES, P, PACK], BF16, name="t_grouped", align_bytes=64)
-            nc.scalar.copy(out=t_grouped[:], in_=turned[:].rearrange("p g j n -> p g n j"))
+            for g2 in range(PASSES):
+                nc.scalar.copy(
+                    out=t_grouped[:, g2, :, :].rearrange("p n (u e) -> p n u e", e=PAIR),
+                    in_=turned[:, g2, :, :].bitcast(BF16).rearrange("p u (n e) -> p n u e", e=PAIR),
+                )
             t_codes[i] = quantised_pool.tile([P, PASSES, P], U32, name="t_codes", align_bytes=64)
             t_scales[i] = quantised_pool.tile([P, PASSES, P], U8, name="t_scales", align_bytes=64)
             nc.vector.quantize_mx(
@@ -166,10 +172,10 @@ def tile_parallelcoattention_kernel(tc, embedding, heatm, W_b_words, W_b_scales,
             return range(0)
 
         for step in range(STEPS + 2):
-            for i in tiles_of(step - 1):
-                turn_and_quantise(i)
             for i in tiles_of(step):
                 first_product(i)
+            for i in tiles_of(step - 1):
+                turn_and_quantise(i)
             for i in tiles_of(step - 2):
                 second_product(i)
 

@@ -102,6 +102,7 @@ def tile_parallelcoattention_kernel(tc, embedding, heatm, W_b_words, W_b_scales,
                 )
 
         t_sorted = {}
+        t_grouped = {}
         t_codes = {}
         t_scales = {}
 
@@ -126,25 +127,29 @@ def tile_parallelcoattention_kernel(tc, embedding, heatm, W_b_words, W_b_scales,
                     in_=t_sum[:].rearrange("n (p u e) -> n u p e", u=PAIRS, e=PAIR),
                 )
 
-        def turn_and_quantise(i):
+        def turn(i):
             turned = turned_psum.tile([P, PASSES, PAIRS, P], F32, name="turned")
             for g2 in range(PASSES):
                 for u in range(PAIRS):
                     nc.tensor.transpose(
                         turned[:, g2, u, :], t_sorted[i][:, g2, u, :].bitcast(F32), ident_f32[:]
                     )
-            t_grouped = grouped_pool.tile([P, PASSES, P, PACK], BF16, name="t_grouped", align_bytes=64)
+            t_grouped[i] = grouped_pool.tile(
+                [P, PASSES, P, PACK], BF16, name="t_grouped", align_bytes=64
+            )
             for g2 in range(PASSES):
                 nc.scalar.copy(
-                    out=t_grouped[:, g2, :, :].rearrange("p n (u e) -> p n u e", e=PAIR),
+                    out=t_grouped[i][:, g2, :, :].rearrange("p n (u e) -> p n u e", e=PAIR),
                     in_=turned[:, g2, :, :].bitcast(BF16).rearrange("p u (n e) -> p n u e", e=PAIR),
                 )
+
+        def quantise_t(i):
             t_codes[i] = quantised_pool.tile([P, PASSES, P], U32, name="t_codes", align_bytes=64)
             t_scales[i] = quantised_pool.tile([P, PASSES, P], U8, name="t_scales", align_bytes=64)
             nc.vector.quantize_mx(
                 out=t_codes[i][:].rearrange("p g n -> p (g n)").bitcast(FP8X4),
                 scales=t_scales[i][:].rearrange("p g n -> p (g n)"),
-                in_=t_grouped[:].rearrange("p g n j -> p (g n j)"),
+                in_=t_grouped[i][:].rearrange("p g n j -> p (g n j)"),
             )
 
         def second_product(i):
@@ -174,10 +179,15 @@ def tile_parallelcoattention_kernel(tc, embedding, heatm, W_b_words, W_b_scales,
         for step in range(STEPS + 2):
             for i in tiles_of(step):
                 first_product(i)
-            for i in tiles_of(step - 1):
-                turn_and_quantise(i)
-            for i in tiles_of(step - 2):
-                second_product(i)
+            turning = tiles_of(step - 1)
+            multiplying = tiles_of(step - 2)
+            for i in turning:
+                turn(i)
+            for k in range(STEP_TILES):
+                if multiplying:
+                    second_product(multiplying[k])
+                if turning:
+                    quantise_t(turning[k])
 
         partition_max = keep.tile([P, 1], F32)
         nc.vector.tensor_reduce(out=partition_max[:], in_=half_max[:], axis=AXIS_X, op=ALU.max)

@@ -15,8 +15,6 @@ AXIS_X = mybir.AxisListType.X
 
 P = 128
 PACK = 4
-PAIR = 2
-PAIRS = PACK // PAIR
 K_PASS = P * PACK
 D = 1024
 N = 1024
@@ -25,10 +23,11 @@ BANK = 512
 HALVES = N // BANK
 ROW_TILES = N // P
 RUN = 4
-STEP_TILES = 2
-STEPS = ROW_TILES // STEP_TILES
-STEP_COLS = STEP_TILES * P
-SUM_BANKS = 6
+CHUNK_TILES = 2
+CHUNKS = ROW_TILES // CHUNK_TILES
+CHUNK_COLS = CHUNK_TILES * P
+PSUM_BANKS = 8
+LEAD = 3
 
 FLOPS = 2 * 2 * N * D * N
 BYTES = 2 * D * N + D * D + D * D // 32 + 4 * N
@@ -39,159 +38,198 @@ def tile_parallelcoattention_kernel(tc, embedding, heatm, W_b_words, W_b_scales,
     with ExitStack() as ctx:
         ctx.enter_context(tc.manual_schedule())
         keep = ctx.enter_context(tc.tile_pool(name="keep", bufs=1))
-        sorted_pool = ctx.enter_context(tc.tile_pool(name="sorted", bufs=2 * STEP_TILES))
-        grouped_pool = ctx.enter_context(tc.tile_pool(name="grouped", bufs=2 * STEP_TILES))
-        quantised_pool = ctx.enter_context(tc.tile_pool(name="quantised", bufs=2 * STEP_TILES))
-        sum_psum = ctx.enter_context(tc.psum_pool(name="sum_psum", bufs=SUM_BANKS))
-        turned_psum = ctx.enter_context(tc.psum_pool(name="turned_psum", bufs=STEP_TILES))
+        t_pool = ctx.enter_context(tc.tile_pool(name="t_pool", bufs=ROW_TILES))
+        banks = ctx.enter_context(tc.psum_pool(name="banks", bufs=PSUM_BANKS))
 
         e_raw = keep.tile([P, PASSES, PACK, N], BF16)
         e_grouped = keep.tile([P, PASSES, N, PACK], BF16, align_bytes=64)
         e_codes = keep.tile([P, PASSES, N], U32, align_bytes=64)
         e_scales = keep.tile([P, PASSES, N], U8, align_bytes=64)
-        w_codes = keep.tile([P, PASSES, D], U32, align_bytes=64)
-        w_scales = keep.tile([P, PASSES, D], U8, align_bytes=64)
+        w_raw = [keep.tile([P, PASSES, BANK], I32, name="w_raw%d" % h, align_bytes=64) for h in range(HALVES)]
+        w_codes = [
+            keep.tile([P, PASSES, PACK, P], I32, name="w_codes%d" % h, align_bytes=64) for h in range(HALVES)
+        ]
+        ws_raw = keep.tile([P, D], U8, align_bytes=64)
+        ws = [keep.tile([P, PACK, P], U8, name="ws%d" % h, align_bytes=64) for h in range(HALVES)]
         ident_f32 = keep.tile([P, P], F32)
         half_max = keep.tile([P, ROW_TILES * HALVES], F32)
         exp_padded = keep.tile([P, P], F32)
         ones = keep.tile([P, P], F32)
         table_warm = keep.tile([P, 1], F32)
 
-        nc.vector.memset(w_scales[:].bitcast(I32), 0)
+        nc.vector.memset(ws_raw[:].bitcast(I32), 0)
         nc.vector.memset(exp_padded[:], 0.0)
         nc.vector.memset(table_warm[:], 0.0)
         nc.vector.memset(ones[:], 1.0)
         nc.scalar.activation(out=table_warm[:], in_=table_warm[:], func=ACT.Tanh)
         make_identity(nc, ident_f32[:])
 
-        def load_embedding(step):
-            cols = slice(step * STEP_COLS, (step + 1) * STEP_COLS)
+        def chunk_cols(q):
+            return slice(q * CHUNK_COLS, (q + 1) * CHUNK_COLS)
+
+        def load_embedding(q):
             for g in range(PASSES):
-                rows = embedding[0, g * K_PASS : (g + 1) * K_PASS, cols]
+                rows = embedding[0, g * K_PASS : (g + 1) * K_PASS, chunk_cols(q)]
                 nc.sync.dma_start(
-                    out=e_raw[:, g, :, cols], in_=rows.rearrange("(p j) n -> p j n", j=PACK)
+                    out=e_raw[:, g, :, chunk_cols(q)],
+                    in_=rows.rearrange("(p j) n -> p j n", j=PACK),
                 )
 
-        load_embedding(0)
-        for r in range(4):
+        def load_w(h):
+            cols = slice(h * BANK, (h + 1) * BANK)
             nc.sync.dma_start(
-                out=w_scales[r:P:32, :, :].bitcast(I32),
-                in_=W_b_scales[:, r:16:4, :].rearrange("g q n -> q g n").bitcast(I32),
-            )
-        for half in range(HALVES):
-            cols = slice(half * BANK, (half + 1) * BANK)
-            nc.sync.dma_start(
-                out=w_codes[:, :, cols].bitcast(I32),
+                out=w_raw[h][:],
                 in_=W_b_words[:, :, cols, :].rearrange("g p n j -> p g (n j)").bitcast(I32),
             )
-        for step in range(1, STEPS):
-            load_embedding(step)
 
-        for step in range(STEPS):
-            cols = slice(step * STEP_COLS, (step + 1) * STEP_COLS)
-            for g in range(PASSES):
-                nc.vector.tensor_copy(
-                    out=e_grouped[:, g, cols, :].rearrange("p (c i) j -> p c j i", i=RUN),
-                    in_=e_raw[:, g, :, cols].rearrange("p j (c i) -> p c j i", i=RUN),
-                )
-            for g in range(PASSES):
-                nc.vector.quantize_mx(
-                    out=e_codes[:, g, cols].bitcast(FP8X4),
-                    scales=e_scales[:, g, cols],
-                    in_=e_grouped[:, g, cols, :].rearrange("p n j -> p (n j)"),
-                )
+        load_embedding(0)
+        for quadrant in range(4):
+            nc.sync.dma_start(
+                out=ws_raw[32 * quadrant : 32 * quadrant + 4 * PASSES, :].bitcast(I32),
+                in_=W_b_scales[:, 4 * quadrant : 4 * quadrant + 4, :].bitcast(I32),
+            )
+        load_w(0)
+        load_w(1)
+        for q in range(1, CHUNKS):
+            load_embedding(q)
 
-        t_sorted = {}
+        def interleave(q, g, copy):
+            copy(
+                out=e_grouped[:, g, chunk_cols(q), :].rearrange("p (c i) j -> p c j i", i=RUN),
+                in_=e_raw[:, g, :, chunk_cols(q)].rearrange("p j (c i) -> p c j i", i=RUN),
+            )
+
+        def quantise_e(q, g):
+            nc.vector.quantize_mx(
+                out=e_codes[:, g, chunk_cols(q)].bitcast(FP8X4),
+                scales=e_scales[:, g, chunk_cols(q)],
+                in_=e_grouped[:, g, chunk_cols(q), :].rearrange("p n j -> p (n j)"),
+            )
+
+        def permute_w(h):
+            nc.vector.tensor_copy(
+                out=w_codes[h][:], in_=w_raw[h][:].rearrange("p g (m j) -> p g j m", j=PACK)
+            )
+
+        def permute_scales(h):
+            nc.vector.tensor_copy(
+                out=ws[h][:],
+                in_=ws_raw[:, h * BANK : (h + 1) * BANK].rearrange("p (m j) -> p j m", j=PACK),
+            )
+
+        t_sum = {}
         t_grouped = {}
         t_codes = {}
         t_scales = {}
+        copied = []
 
-        def first_product(i):
-            rows = slice(i * P, (i + 1) * P)
-            t_sorted[i] = sorted_pool.tile([P, PASSES, PAIRS, P * PAIR], BF16, name="t_sorted")
-            for g2 in range(PASSES):
-                cols = slice(g2 * BANK, (g2 + 1) * BANK)
-                t_sum = sum_psum.tile([P, BANK], F32, name="t_sum", tag="sum")
+        def first_product(c, h):
+            rows = slice(c * P, (c + 1) * P)
+            t_sum[c, h] = banks.tile([P, PACK, P], F32, name="t_sum", tag="bank")
+            for j in range(PACK):
                 for g in range(PASSES):
                     nc.tensor.matmul_mx(
-                        out=t_sum[:],
-                        lhsT=e_codes[:, g, rows].bitcast(FP8X4),
-                        lhsT_scale=e_scales[:, g, rows],
-                        rhs=w_codes[:, g, cols].bitcast(FP8X4),
-                        rhs_scale=w_scales[:, g, cols],
+                        out=t_sum[c, h][:, j, :],
+                        lhsT=w_codes[h][:, g, j, :].bitcast(FP8X4),
+                        lhsT_scale=ws[h][4 * g : P, j, :],
+                        rhs=e_codes[:, g, rows].bitcast(FP8X4),
+                        rhs_scale=e_scales[:, g, rows],
                         start=(g == 0),
                         stop=(g == PASSES - 1),
                     )
-                nc.scalar.copy(
-                    out=t_sorted[i][:, g2, :, :].rearrange("n u (p e) -> n u p e", e=PAIR),
-                    in_=t_sum[:].rearrange("n (p u e) -> n u p e", u=PAIRS, e=PAIR),
-                )
 
-        def turn(i):
-            turned = turned_psum.tile([P, PASSES, PAIRS, P], F32, name="turned")
-            for g2 in range(PASSES):
-                for u in range(PAIRS):
-                    nc.tensor.transpose(
-                        turned[:, g2, u, :], t_sorted[i][:, g2, u, :].bitcast(F32), ident_f32[:]
-                    )
-            t_grouped[i] = grouped_pool.tile(
-                [P, PASSES, P, PACK], BF16, name="t_grouped", align_bytes=64
+        def copy_out(c, h):
+            if h == 0:
+                t_grouped[c] = t_pool.tile(
+                    [P, HALVES, P, PACK], BF16, name="t_grouped", align_bytes=64
+                )
+            nc.scalar.copy(
+                out=t_grouped[c][:, h, :, :], in_=t_sum[c, h][:].rearrange("p j n -> p n j")
             )
-            for g2 in range(PASSES):
-                nc.scalar.copy(
-                    out=t_grouped[i][:, g2, :, :].rearrange("p n (u e) -> p n u e", e=PAIR),
-                    in_=turned[:, g2, :, :].bitcast(BF16).rearrange("p u (n e) -> p n u e", e=PAIR),
-                )
+            if h == HALVES - 1:
+                copied.append(c)
 
-        def quantise_t(i):
-            t_codes[i] = quantised_pool.tile([P, PASSES, P], U32, name="t_codes", align_bytes=64)
-            t_scales[i] = quantised_pool.tile([P, PASSES, P], U8, name="t_scales", align_bytes=64)
+        def quantise_t(c):
+            t_codes[c] = t_pool.tile([P, HALVES, P], U32, name="t_codes", align_bytes=64)
+            t_scales[c] = t_pool.tile([P, HALVES, P], U8, name="t_scales", align_bytes=64)
             nc.vector.quantize_mx(
-                out=t_codes[i][:].rearrange("p g n -> p (g n)").bitcast(FP8X4),
-                scales=t_scales[i][:].rearrange("p g n -> p (g n)"),
-                in_=t_grouped[i][:].rearrange("p g n j -> p (g n j)"),
+                out=t_codes[c][:].rearrange("p g n -> p (g n)").bitcast(FP8X4),
+                scales=t_scales[c][:].rearrange("p g n -> p (g n)"),
+                in_=t_grouped[c][:].rearrange("p g n j -> p (g n j)"),
             )
 
-        def second_product(i):
+        def quantise_next():
+            if copied:
+                quantise_t(copied[0])
+                copied.remove(copied[0])
+
+        def second_product(c):
             for half in range(HALVES):
                 cols = slice(half * BANK, (half + 1) * BANK)
-                c_sum = sum_psum.tile([P, BANK], F32, name="c_sum", tag="sum")
+                c_sum = banks.tile([P, BANK], F32, name="c_sum", tag="bank")
                 for g2 in range(PASSES):
                     nc.tensor.matmul_mx(
                         out=c_sum[:],
-                        lhsT=t_codes[i][:, g2, :].bitcast(FP8X4),
-                        lhsT_scale=t_scales[i][:, g2, :],
+                        lhsT=t_codes[c][:, g2, :].bitcast(FP8X4),
+                        lhsT_scale=t_scales[c][:, g2, :],
                         rhs=e_codes[:, g2, cols].bitcast(FP8X4),
                         rhs_scale=e_scales[:, g2, cols],
                         start=(g2 == 0),
                         stop=(g2 == PASSES - 1),
                     )
-                place = i * HALVES + half
+                place = c * HALVES + half
                 nc.vector.tensor_reduce(
                     out=half_max[:, place : place + 1], in_=c_sum[:], axis=AXIS_X, op=ALU.max
                 )
 
-        def tiles_of(step):
-            if 0 <= step < STEPS:
-                return range(step * STEP_TILES, (step + 1) * STEP_TILES)
-            return range(0)
+        interleave(0, 0, nc.vector.tensor_copy)
+        interleave(0, 1, nc.scalar.copy)
+        permute_scales(0)
+        quantise_e(0, 0)
+        permute_w(0)
+        quantise_e(0, 1)
+        for c in (0, 1):
+            first_product(c, 0)
+        permute_scales(1)
+        permute_w(1)
+        for c in (0, 1):
+            first_product(c, 1)
 
-        for step in range(STEPS + 2):
-            for i in tiles_of(step):
-                first_product(i)
-            turning = tiles_of(step - 1)
-            multiplying = tiles_of(step - 2)
-            for i in turning:
-                turn(i)
-            for k in range(STEP_TILES):
-                if multiplying:
-                    second_product(multiplying[k])
-                if turning:
-                    quantise_t(turning[k])
+        for q in range(1, CHUNKS):
+            interleave(q, 0, nc.vector.tensor_copy)
+            interleave(q, 1, nc.scalar.copy if q < CHUNKS - 1 else nc.vector.tensor_copy)
+            if q > 1:
+                quantise_e(q - 1, 1)
+            quantise_e(q, 0)
+            if q <= HALVES:
+                for c in (0, 1):
+                    copy_out(c, q - 1)
+        quantise_e(CHUNKS - 1, 1)
+        for h in range(HALVES):
+            for c in (2, 3):
+                first_product(c, h)
+        quantise_next()
+        quantise_next()
+        for h in range(HALVES):
+            for c in (2, 3):
+                copy_out(c, h)
+
+        later = [(c, h) for c in range(4, ROW_TILES) for h in range(HALVES)]
+        for c, h in later[:LEAD]:
+            first_product(c, h)
+            copy_out(c, h)
+        for c in range(ROW_TILES):
+            if c not in t_codes:
+                quantise_next()
+            second_product(c)
+            quantise_next()
+            for c1, h1 in later[LEAD + c : LEAD + c + 1]:
+                first_product(c1, h1)
+                copy_out(c1, h1)
 
         partition_max = keep.tile([P, 1], F32)
         nc.vector.tensor_reduce(out=partition_max[:], in_=half_max[:], axis=AXIS_X, op=ALU.max)
-        max_spread = sum_psum.tile([P, P], F32, name="max_spread", tag="sum")
+        max_spread = banks.tile([P, P], F32, name="max_spread", tag="bank")
         nc.tensor.transpose(max_spread[:], partition_max[:, 0:1].to_broadcast([P, P]), ident_f32[:])
         row_max = keep.tile([P, ROW_TILES], F32)
         nc.vector.tensor_reduce(
@@ -214,9 +252,9 @@ def tile_parallelcoattention_kernel(tc, embedding, heatm, W_b_words, W_b_scales,
             bias=minus_top[:, 0:1],
             accum_out=partition_sum[:],
         )
-        exp_turned = sum_psum.tile([P, P], F32, name="exp_turned", tag="sum")
+        exp_turned = banks.tile([P, P], F32, name="exp_turned", tag="bank")
         nc.tensor.transpose(exp_turned[:], exp_padded[:], ident_f32[:])
-        total = sum_psum.tile([P, 1], F32, name="total", tag="sum")
+        total = banks.tile([P, 1], F32, name="total", tag="bank")
         nc.tensor.matmul(out=total[:], lhsT=ones[:], rhs=partition_sum[:], start=True, stop=True)
         inverse = keep.tile([P, 1], F32)
         nc.vector.reciprocal(out=inverse[:], in_=total[:])

@@ -41,7 +41,11 @@ def tile_parallelcoattention_kernel(tc, embedding, heatm, W_b_words, W_b_scales,
         t_pool = ctx.enter_context(tc.tile_pool(name="t_pool", bufs=ROW_TILES))
         banks = ctx.enter_context(tc.psum_pool(name="banks", bufs=PSUM_BANKS))
 
-        e_raw = keep.tile([P, PASSES, PACK, N], BF16)
+        e_raw = {
+            (q, g): keep.tile([P, PACK, CHUNK_COLS], BF16, name="e_raw%d%d" % (q, g))
+            for q in range(CHUNKS)
+            for g in range(PASSES)
+        }
         e_grouped = keep.tile([P, PASSES, N, PACK], BF16, align_bytes=64)
         e_codes = keep.tile([P, PASSES, N], U32, align_bytes=64)
         e_scales = keep.tile([P, PASSES, N], U8, align_bytes=64)
@@ -64,23 +68,18 @@ def tile_parallelcoattention_kernel(tc, embedding, heatm, W_b_words, W_b_scales,
         nc.scalar.activation(out=table_warm[:], in_=table_warm[:], func=ACT.Tanh)
         make_identity(nc, ident_f32[:])
 
-        def chunk_cols(q):
-            return slice(q * CHUNK_COLS, (q + 1) * CHUNK_COLS)
-
         def load_embedding(q):
             for g in range(PASSES):
-                rows = embedding[0, g * K_PASS : (g + 1) * K_PASS, chunk_cols(q)]
-                nc.sync.dma_start(
-                    out=e_raw[:, g, :, chunk_cols(q)],
-                    in_=rows.rearrange("(p j) n -> p j n", j=PACK),
-                )
+                rows = embedding[0, g * K_PASS : (g + 1) * K_PASS, q * CHUNK_COLS : (q + 1) * CHUNK_COLS]
+                nc.sync.dma_start(out=e_raw[q, g][:], in_=rows.rearrange("(p j) n -> p j n", j=PACK))
 
         def load_w(h):
             cols = slice(h * BANK, (h + 1) * BANK)
-            nc.sync.dma_start(
-                out=w_raw[h][:],
-                in_=W_b_words[:, :, cols, :].rearrange("g p n j -> p g (n j)").bitcast(I32),
-            )
+            for g in range(PASSES):
+                nc.sync.dma_start(
+                    out=w_raw[h][:, g, :],
+                    in_=W_b_words[g, :, cols, :].rearrange("p n j -> p (n j)").bitcast(I32),
+                )
 
         load_embedding(0)
         for quadrant in range(4):
@@ -93,22 +92,26 @@ def tile_parallelcoattention_kernel(tc, embedding, heatm, W_b_words, W_b_scales,
         for q in range(1, CHUNKS):
             load_embedding(q)
 
-        def interleave(q, g, copy):
+        def interleave(first, tiles, g, copy):
+            q = first // CHUNK_TILES
+            cols = slice(first * P, (first + tiles) * P)
+            local = slice(first * P - q * CHUNK_COLS, (first + tiles) * P - q * CHUNK_COLS)
             copy(
-                out=e_grouped[:, g, chunk_cols(q), :].rearrange("p (c i) j -> p c j i", i=RUN),
-                in_=e_raw[:, g, :, chunk_cols(q)].rearrange("p j (c i) -> p c j i", i=RUN),
+                out=e_grouped[:, g, cols, :].rearrange("p (c i) j -> p c j i", i=RUN),
+                in_=e_raw[q, g][:, :, local].rearrange("p j (c i) -> p c j i", i=RUN),
             )
 
-        def quantise_e(q, g):
+        def quantise_e(first, tiles, g):
+            cols = slice(first * P, (first + tiles) * P)
             nc.vector.quantize_mx(
-                out=e_codes[:, g, chunk_cols(q)].bitcast(FP8X4),
-                scales=e_scales[:, g, chunk_cols(q)],
-                in_=e_grouped[:, g, chunk_cols(q), :].rearrange("p n j -> p (n j)"),
+                out=e_codes[:, g, cols].bitcast(FP8X4),
+                scales=e_scales[:, g, cols],
+                in_=e_grouped[:, g, cols, :].rearrange("p n j -> p (n j)"),
             )
 
-        def permute_w(h):
+        def permute_w(h, g):
             nc.vector.tensor_copy(
-                out=w_codes[h][:], in_=w_raw[h][:].rearrange("p g (m j) -> p g j m", j=PACK)
+                out=w_codes[h][:, g, :, :], in_=w_raw[h][:, g, :].rearrange("p (m j) -> p j m", j=PACK)
             )
 
         def permute_scales(h):
@@ -182,34 +185,45 @@ def tile_parallelcoattention_kernel(tc, embedding, heatm, W_b_words, W_b_scales,
                     out=half_max[:, place : place + 1], in_=c_sum[:], axis=AXIS_X, op=ALU.max
                 )
 
-        interleave(0, 0, nc.vector.tensor_copy)
-        interleave(0, 1, nc.scalar.copy)
+        interleave(0, 2, 0, nc.vector.tensor_copy)
+        interleave(0, 2, 1, nc.scalar.copy)
         permute_scales(0)
-        quantise_e(0, 0)
-        permute_w(0)
-        quantise_e(0, 1)
+        permute_scales(1)
+        quantise_e(0, 2, 0)
+        permute_w(0, 0)
+        permute_w(0, 1)
+        quantise_e(0, 2, 1)
         for c in (0, 1):
             first_product(c, 0)
-        permute_scales(1)
-        permute_w(1)
+        permute_w(1, 0)
+        permute_w(1, 1)
         for c in (0, 1):
             first_product(c, 1)
 
-        for q in range(1, CHUNKS):
-            interleave(q, 0, nc.vector.tensor_copy)
-            interleave(q, 1, nc.scalar.copy if q < CHUNKS - 1 else nc.vector.tensor_copy)
-            if q > 1:
-                quantise_e(q - 1, 1)
-            quantise_e(q, 0)
-            if q <= HALVES:
-                for c in (0, 1):
-                    copy_out(c, q - 1)
-        quantise_e(CHUNKS - 1, 1)
+        for g in range(PASSES):
+            interleave(2, 1, g, nc.vector.tensor_copy)
+            interleave(3, 1, g, nc.scalar.copy)
+            quantise_e(2, 1, g)
+        for g in range(PASSES):
+            quantise_e(3, 1, g)
+        for c in (0, 1):
+            copy_out(c, 0)
         for h in range(HALVES):
             for c in (2, 3):
                 first_product(c, h)
+
+        interleave(4, 2, 0, nc.vector.tensor_copy)
+        interleave(4, 2, 1, nc.vector.tensor_copy)
+        for c in (0, 1):
+            copy_out(c, 1)
+        quantise_e(4, 2, 0)
+        quantise_e(4, 2, 1)
+        interleave(6, 2, 0, nc.vector.tensor_copy)
+        interleave(6, 2, 1, nc.scalar.copy)
         quantise_next()
         quantise_next()
+        quantise_e(6, 2, 0)
+        quantise_e(6, 2, 1)
         for h in range(HALVES):
             for c in (2, 3):
                 copy_out(c, h)

@@ -28,6 +28,7 @@ CHUNKS = ROW_TILES // CHUNK_TILES
 CHUNK_COLS = CHUNK_TILES * P
 PSUM_BANKS = 8
 LEAD = 3
+IDLE_RUN = 4
 
 FLOPS = 2 * 2 * N * D * N
 BYTES = 2 * D * N + D * D + D * D // 32 + 4 * N
@@ -60,8 +61,12 @@ def tile_parallelcoattention_kernel(tc, embedding, heatm, W_b_words, W_b_scales,
         exp_padded = keep.tile([P, P], F32)
         ones = keep.tile([P, P], F32)
         table_warm = keep.tile([P, 1], F32)
+        idle_weights = keep.tile([P, P], BF16)
+        idle_columns = keep.tile([P, BANK], BF16)
 
         nc.vector.memset(ws_raw[:].bitcast(I32), 0)
+        nc.vector.memset(idle_weights[:], 0.0)
+        nc.vector.memset(idle_columns[:], 0.0)
         nc.vector.memset(exp_padded[:], 0.0)
         nc.vector.memset(table_warm[:], 0.0)
         nc.vector.memset(ones[:], 1.0)
@@ -185,7 +190,15 @@ def tile_parallelcoattention_kernel(tc, embedding, heatm, W_b_words, W_b_scales,
                     out=half_max[:, place : place + 1], in_=c_sum[:], axis=AXIS_X, op=ALU.max
                 )
 
+        idle_sum = banks.tile([P, BANK], F32, name="idle_sum", tag="bank")
+
+        def keep_busy(columns):
+            for i in range(IDLE_RUN):
+                nc.tensor.matmul(out=idle_sum[:], lhsT=idle_weights[:], rhs=columns, start=True, stop=True)
+
+        keep_busy(idle_columns[:])
         interleave(0, 2, 0, nc.vector.tensor_copy)
+        keep_busy(e_grouped[:, 0, 0:P, :].rearrange("p n j -> p (n j)"))
         interleave(0, 2, 1, nc.scalar.copy)
         permute_scales(0)
         permute_scales(1)

@@ -197,7 +197,7 @@ def tile_parallelcoattention_kernel(tc, embedding, heatm, W_b_words, W_b_scales,
                 nc.tensor.matmul(out=idle_sum[:], lhsT=idle_weights[:], rhs=columns, start=True, stop=True)
 
         keep_busy(idle_columns[:])
-        interleave(0, 2, 0, nc.vector.tensor_copy)
+        interleave(0, 2, 0, nc.scalar.copy)
         keep_busy(e_grouped[:, 0, 0:P, :].rearrange("p n j -> p (n j)"))
         interleave(0, 2, 1, nc.scalar.copy)
         permute_scales(0)
@@ -231,7 +231,7 @@ def tile_parallelcoattention_kernel(tc, embedding, heatm, W_b_words, W_b_scales,
             copy_out(c, 1)
         quantise_e(4, 2, 0)
         quantise_e(4, 2, 1)
-        interleave(6, 2, 0, nc.vector.tensor_copy)
+        interleave(6, 2, 0, nc.scalar.copy)
         interleave(6, 2, 1, nc.scalar.copy)
         quantise_next()
         quantise_next()

@@ -47,15 +47,15 @@ def tile_parallelcoattention_kernel(tc, embedding, heatm, W_b_words, W_b_scales,
             for q in range(CHUNKS)
             for g in range(PASSES)
         }
-        e_grouped = keep.tile([P, PASSES, N, PACK], BF16, align_bytes=64)
-        e_codes = keep.tile([P, PASSES, N], U32, align_bytes=64)
-        e_scales = keep.tile([P, PASSES, N], U8, align_bytes=64)
-        w_raw = [keep.tile([P, PASSES, BANK], I32, name="w_raw%d" % h, align_bytes=64) for h in range(HALVES)]
+        e_grouped = keep.tile([P, PASSES, N, PACK], BF16, align_bytes=256)
+        e_codes = keep.tile([P, PASSES, N], U32, align_bytes=256)
+        e_scales = keep.tile([P, PASSES, N], U8, align_bytes=256)
+        w_raw = [keep.tile([P, PASSES, BANK], I32, name="w_raw%d" % h, align_bytes=256) for h in range(HALVES)]
         w_codes = [
-            keep.tile([P, PASSES, PACK, P], I32, name="w_codes%d" % h, align_bytes=64) for h in range(HALVES)
+            keep.tile([P, PASSES, PACK, P], I32, name="w_codes%d" % h, align_bytes=256) for h in range(HALVES)
         ]
-        ws_raw = keep.tile([P, D], U8, align_bytes=64)
-        ws = [keep.tile([P, PACK, P], U8, name="ws%d" % h, align_bytes=64) for h in range(HALVES)]
+        ws_raw = keep.tile([P, D], U8, align_bytes=256)
+        ws = [keep.tile([P, PACK, P], U8, name="ws%d" % h, align_bytes=256) for h in range(HALVES)]
         ident_f32 = keep.tile([P, P], F32)
         half_max = keep.tile([P, ROW_TILES * HALVES], F32)
         exp_padded = keep.tile([P, P], F32)
@@ -149,7 +149,7 @@ def tile_parallelcoattention_kernel(tc, embedding, heatm, W_b_words, W_b_scales,
         def copy_out(c, h):
             if h == 0:
                 t_grouped[c] = t_pool.tile(
-                    [P, HALVES, P, PACK], BF16, name="t_grouped", align_bytes=64
+                    [P, HALVES, P, PACK], BF16, name="t_grouped", align_bytes=256
                 )
             nc.scalar.copy(
                 out=t_grouped[c][:, h, :, :], in_=t_sum[c, h][:].rearrange("p j n -> p n j")
@@ -158,8 +158,8 @@ def tile_parallelcoattention_kernel(tc, embedding, heatm, W_b_words, W_b_scales,
                 copied.append(c)
 
         def quantise_t(c):
-            t_codes[c] = t_pool.tile([P, HALVES, P], U32, name="t_codes", align_bytes=64)
-            t_scales[c] = t_pool.tile([P, HALVES, P], U8, name="t_scales", align_bytes=64)
+            t_codes[c] = t_pool.tile([P, HALVES, P], U32, name="t_codes", align_bytes=256)
+            t_scales[c] = t_pool.tile([P, HALVES, P], U8, name="t_scales", align_bytes=256)
             nc.vector.quantize_mx(
                 out=t_codes[c][:].rearrange("p g n -> p (g n)").bitcast(FP8X4),
                 scales=t_scales[c][:].rearrange("p g n -> p (g n)"),

@@ -29,6 +29,7 @@ CHUNK_COLS = CHUNK_TILES * P
 PSUM_BANKS = 8
 LEAD = 3
 IDLE_RUN = 4
+LINE = 16
 
 FLOPS = 2 * 2 * N * D * N
 BYTES = 2 * D * N + D * D + D * D // 32 + 4 * N
@@ -116,13 +117,14 @@ def tile_parallelcoattention_kernel(tc, embedding, heatm, W_b_words, W_b_scales,
 
         def permute_w(h, g):
             nc.vector.tensor_copy(
-                out=w_codes[h][:, g, :, :], in_=w_raw[h][:, g, :].rearrange("p (m j) -> p j m", j=PACK)
+                out=w_codes[h][:, g, :, :].rearrange("p j (c i) -> p c j i", i=LINE // 4),
+                in_=w_raw[h][:, g, :].rearrange("p (c i j) -> p c j i", i=LINE // 4, j=PACK),
             )
 
         def permute_scales(h):
             nc.vector.tensor_copy(
-                out=ws[h][:],
-                in_=ws_raw[:, h * BANK : (h + 1) * BANK].rearrange("p (m j) -> p j m", j=PACK),
+                out=ws[h][:].rearrange("p j (c i) -> p c j i", i=LINE),
+                in_=ws_raw[:, h * BANK : (h + 1) * BANK].rearrange("p (c i j) -> p c j i", i=LINE, j=PACK),
             )
 
         t_sum = {}

@@ -23,12 +23,9 @@ BANK = 512
 HALVES = N // BANK
 ROW_TILES = N // P
 RUN = 4
-CHUNK_TILES = 2
-CHUNKS = ROW_TILES // CHUNK_TILES
-CHUNK_COLS = CHUNK_TILES * P
+CHUNKS = ((0, 2), (2, 2), (4, 2), (6, 2))
 PSUM_BANKS = 8
 LEAD = 3
-IDLE_RUN = 4
 LINE = 16
 
 FLOPS = 2 * 2 * N * D * N
@@ -44,8 +41,8 @@ def tile_parallelcoattention_kernel(tc, embedding, heatm, W_b_words, W_b_scales,
         banks = ctx.enter_context(tc.psum_pool(name="banks", bufs=PSUM_BANKS))
 
         e_raw = {
-            (q, g): keep.tile([P, PACK, CHUNK_COLS], BF16, name="e_raw%d%d" % (q, g))
-            for q in range(CHUNKS)
+            (q, g): keep.tile([P, PACK, tiles * P], BF16, name="e_raw%d%d" % (q, g))
+            for q, (first, tiles) in enumerate(CHUNKS)
             for g in range(PASSES)
         }
         e_grouped = keep.tile([P, PASSES, N, PACK], BF16, align_bytes=256)
@@ -59,7 +56,9 @@ def tile_parallelcoattention_kernel(tc, embedding, heatm, W_b_words, W_b_scales,
         ws = [keep.tile([P, PACK, P], U8, name="ws%d" % h, align_bytes=256) for h in range(HALVES)]
         ident_f32 = keep.tile([P, P], F32)
         half_max = keep.tile([P, ROW_TILES * HALVES], F32)
-        exp_padded = keep.tile([P, P], F32)
+        minus_tanh = keep.tile([P, ROW_TILES * HALVES], F32)
+        minus_m = keep.tile([P, P], F32)
+        tile_sum = keep.tile([P, 1], F32)
         ones = keep.tile([P, P], F32)
         table_warm = keep.tile([P, 1], F32)
         idle_weights = keep.tile([P, P], BF16)
@@ -68,16 +67,12 @@ def tile_parallelcoattention_kernel(tc, embedding, heatm, W_b_words, W_b_scales,
         nc.vector.memset(ws_raw[:].bitcast(I32), 0)
         nc.vector.memset(idle_weights[:], 0.0)
         nc.vector.memset(idle_columns[:], 0.0)
-        nc.vector.memset(exp_padded[:], 0.0)
+        nc.vector.memset(minus_m[:], 0.0)
+        nc.vector.memset(tile_sum[:], 0.0)
         nc.vector.memset(table_warm[:], 0.0)
         nc.vector.memset(ones[:], 1.0)
         nc.scalar.activation(out=table_warm[:], in_=table_warm[:], func=ACT.Tanh)
         make_identity(nc, ident_f32[:])
-
-        def load_embedding(q):
-            for g in range(PASSES):
-                rows = embedding[0, g * K_PASS : (g + 1) * K_PASS, q * CHUNK_COLS : (q + 1) * CHUNK_COLS]
-                nc.sync.dma_start(out=e_raw[q, g][:], in_=rows.rearrange("(p j) n -> p j n", j=PACK))
 
         def load_w(h):
             cols = slice(h * BANK, (h + 1) * BANK)
@@ -87,21 +82,40 @@ def tile_parallelcoattention_kernel(tc, embedding, heatm, W_b_words, W_b_scales,
                     in_=W_b_words[g, :, cols, :].rearrange("p n j -> p (n j)").bitcast(I32),
                 )
 
-        load_embedding(0)
+        def load_embedding_pass(q, g):
+            first, tiles = CHUNKS[q]
+            rows = embedding[0, g * K_PASS : (g + 1) * K_PASS, first * P : (first + tiles) * P]
+            nc.sync.dma_start(out=e_raw[q, g][:], in_=rows.rearrange("(p j) n -> p j n", j=PACK))
+
+        def load_w_pass(h, g):
+            cols = slice(h * BANK, (h + 1) * BANK)
+            nc.sync.dma_start(
+                out=w_raw[h][:, g, :],
+                in_=W_b_words[g, :, cols, :].rearrange("p n j -> p (n j)").bitcast(I32),
+            )
+
+        load_embedding_pass(0, 0)
         for quadrant in range(4):
             nc.sync.dma_start(
                 out=ws_raw[32 * quadrant : 32 * quadrant + 4 * PASSES, :].bitcast(I32),
                 in_=W_b_scales[:, 4 * quadrant : 4 * quadrant + 4, :].bitcast(I32),
             )
-        load_w(0)
-        load_w(1)
-        for q in range(1, CHUNKS):
-            load_embedding(q)
+        load_embedding_pass(0, 1)
+        load_w_pass(0, 0)
+        load_w_pass(0, 1)
+        load_w_pass(1, 0)
+        load_w_pass(1, 1)
+        load_embedding_pass(1, 0)
+        load_embedding_pass(1, 1)
+        load_embedding_pass(2, 0)
+        load_embedding_pass(2, 1)
+        load_embedding_pass(3, 0)
+        load_embedding_pass(3, 1)
 
         def interleave(first, tiles, g, copy):
-            q = first // CHUNK_TILES
+            q = max(i for i, (start, count) in enumerate(CHUNKS) if start <= first)
             cols = slice(first * P, (first + tiles) * P)
-            local = slice(first * P - q * CHUNK_COLS, (first + tiles) * P - q * CHUNK_COLS)
+            local = slice((first - CHUNKS[q][0]) * P, (first + tiles - CHUNKS[q][0]) * P)
             copy(
                 out=e_grouped[:, g, cols, :].rearrange("p (c i) j -> p c j i", i=RUN),
                 in_=e_raw[q, g][:, :, local].rearrange("p j (c i) -> p c j i", i=RUN),
@@ -194,61 +208,62 @@ def tile_parallelcoattention_kernel(tc, embedding, heatm, W_b_words, W_b_scales,
 
         idle_sum = banks.tile([P, BANK], F32, name="idle_sum", tag="bank")
 
-        def keep_busy(columns):
-            for i in range(IDLE_RUN):
+        def keep_busy(columns, run):
+            for i in range(run):
                 nc.tensor.matmul(out=idle_sum[:], lhsT=idle_weights[:], rhs=columns, start=True, stop=True)
 
-        keep_busy(idle_columns[:])
+        keep_busy(idle_columns[:], 10)
         interleave(0, 2, 0, nc.scalar.copy)
-        keep_busy(e_grouped[:, 0, 0:P, :].rearrange("p n j -> p (n j)"))
-        interleave(0, 2, 1, nc.scalar.copy)
         permute_scales(0)
         permute_scales(1)
+        interleave(0, 2, 1, nc.scalar.copy)
         quantise_e(0, 2, 0)
         permute_w(0, 0)
         permute_w(0, 1)
         quantise_e(0, 2, 1)
-        for c in (0, 1):
-            first_product(c, 0)
+        first_product(0, 0)
+        first_product(1, 0)
         permute_w(1, 0)
         permute_w(1, 1)
-        for c in (0, 1):
-            first_product(c, 1)
-
-        for g in range(PASSES):
-            interleave(2, 1, g, nc.vector.tensor_copy)
-            interleave(3, 1, g, nc.scalar.copy)
-            quantise_e(2, 1, g)
-        for g in range(PASSES):
-            quantise_e(3, 1, g)
-        for c in (0, 1):
-            copy_out(c, 0)
-        for h in range(HALVES):
-            for c in (2, 3):
-                first_product(c, h)
-
+        first_product(0, 1)
+        first_product(1, 1)
+        interleave(2, 1, 0, nc.vector.tensor_copy)
+        interleave(3, 1, 0, nc.scalar.copy)
+        quantise_e(2, 1, 0)
+        interleave(2, 1, 1, nc.vector.tensor_copy)
+        interleave(3, 1, 1, nc.scalar.copy)
+        quantise_e(2, 1, 1)
+        quantise_e(3, 1, 0)
+        quantise_e(3, 1, 1)
+        copy_out(0, 0)
+        copy_out(1, 0)
+        first_product(2, 0)
+        first_product(3, 0)
+        first_product(2, 1)
+        first_product(3, 1)
         interleave(4, 2, 0, nc.vector.tensor_copy)
         interleave(4, 2, 1, nc.vector.tensor_copy)
-        for c in (0, 1):
-            copy_out(c, 1)
+        copy_out(0, 1)
+        copy_out(1, 1)
         quantise_e(4, 2, 0)
         quantise_e(4, 2, 1)
         interleave(6, 2, 0, nc.scalar.copy)
-        interleave(6, 2, 1, nc.scalar.copy)
+        interleave(6, 2, 1, nc.vector.tensor_copy)
         quantise_next()
         quantise_next()
         quantise_e(6, 2, 0)
         quantise_e(6, 2, 1)
-        for h in range(HALVES):
-            for c in (2, 3):
-                copy_out(c, h)
+        copy_out(2, 0)
+        copy_out(3, 0)
+        copy_out(2, 1)
+        copy_out(3, 1)
 
         later = [(c, h) for c in range(4, ROW_TILES) for h in range(HALVES)]
         for c, h in later[:LEAD]:
             first_product(c, h)
             copy_out(c, h)
         for c in range(ROW_TILES):
-            if c not in t_codes:
+            while c not in t_codes:
                 quantise_next()
             second_product(c)
             quantise_next()
@@ -256,39 +271,47 @@ def tile_parallelcoattention_kernel(tc, embedding, heatm, W_b_words, W_b_scales,
                 first_product(c1, h1)
                 copy_out(c1, h1)
 
-        partition_max = keep.tile([P, 1], F32)
-        nc.vector.tensor_reduce(out=partition_max[:], in_=half_max[:], axis=AXIS_X, op=ALU.max)
-        max_spread = banks.tile([P, P], F32, name="max_spread", tag="bank")
-        nc.tensor.transpose(max_spread[:], partition_max[:, 0:1].to_broadcast([P, P]), ident_f32[:])
-        row_max = keep.tile([P, ROW_TILES], F32)
-        nc.vector.tensor_reduce(
-            out=row_max[:],
-            in_=half_max[:].rearrange("p (i h) -> p i h", h=HALVES),
-            axis=AXIS_X,
-            op=ALU.max,
-        )
-        m = keep.tile([P, ROW_TILES], F32)
-        nc.scalar.activation(out=m[:], in_=row_max[:], func=ACT.Tanh)
-        top_argument = keep.tile([P, 1], F32)
-        nc.vector.tensor_reduce(out=top_argument[:], in_=max_spread[:], axis=AXIS_X, op=ALU.max)
-        minus_top = keep.tile([P, 1], F32)
-        nc.scalar.activation(out=minus_top[:], in_=top_argument[:], func=ACT.Tanh, scale=-1.0)
-        partition_sum = keep.tile([P, 1], F32)
+        last = ROW_TILES * HALVES - 1
+        nc.scalar.activation(out=minus_tanh[:, 0:last], in_=half_max[:, 0:last], func=ACT.Tanh, scale=-1.0)
         nc.scalar.activation(
-            out=exp_padded[:, 0:ROW_TILES],
-            in_=m[:],
-            func=ACT.Exp,
-            bias=minus_top[:, 0:1],
-            accum_out=partition_sum[:],
+            out=minus_tanh[:, last : last + 1], in_=half_max[:, last : last + 1], func=ACT.Tanh, scale=-1.0
         )
-        exp_turned = banks.tile([P, P], F32, name="exp_turned", tag="bank")
-        nc.tensor.transpose(exp_turned[:], exp_padded[:], ident_f32[:])
+        earlier_min = keep.tile([P, 1], F32)
+        nc.vector.tensor_reduce(out=earlier_min[:], in_=minus_tanh[:, 0:last], axis=AXIS_X, op=ALU.min)
+        spread = banks.tile([P, 2, P], F32, name="spread", tag="bank")
+        nc.tensor.transpose(spread[:, 0, :], earlier_min[:, 0:1].to_broadcast([P, P]), ident_f32[:])
+        nc.tensor.transpose(
+            spread[:, 1, :], minus_tanh[:, last : last + 1].to_broadcast([P, P]), ident_f32[:]
+        )
+        nc.vector.tensor_reduce(
+            out=minus_m[:, 0:ROW_TILES],
+            in_=minus_tanh[:].rearrange("p (i h) -> p i h", h=HALVES),
+            axis=AXIS_X,
+            op=ALU.min,
+        )
+        minus_m_turned = banks.tile([P, P], F32, name="minus_m_turned", tag="bank")
+        nc.tensor.transpose(minus_m_turned[:], minus_m[:], ident_f32[:])
+        minus_top = keep.tile([P, 1], F32)
+        nc.vector.tensor_reduce(
+            out=minus_top[:], in_=spread[:].rearrange("p a n -> p (a n)"), axis=AXIS_X, op=ALU.min
+        )
+        exps = keep.tile([P, P], F32)
+        nc.scalar.activation(
+            out=exps[0:ROW_TILES, :],
+            in_=minus_m_turned[0:ROW_TILES, :],
+            func=ACT.Exp,
+            scale=-1.0,
+            bias=minus_top[0:ROW_TILES, 0:1],
+            accum_out=tile_sum[0:ROW_TILES, :],
+        )
         total = banks.tile([P, 1], F32, name="total", tag="bank")
-        nc.tensor.matmul(out=total[:], lhsT=ones[:], rhs=partition_sum[:], start=True, stop=True)
+        nc.tensor.matmul(out=total[:], lhsT=ones[:], rhs=tile_sum[:], start=True, stop=True)
         inverse = keep.tile([P, 1], F32)
-        nc.vector.reciprocal(out=inverse[:], in_=total[:])
+        nc.vector.reciprocal(out=inverse[0:ROW_TILES, :], in_=total[0:ROW_TILES, :])
         weights = keep.tile([P, P], F32)
-        nc.vector.tensor_scalar_mul(out=weights[:], in0=exp_turned[:], scalar1=inverse[:, 0:1])
+        nc.vector.tensor_scalar_mul(
+            out=weights[0:ROW_TILES, :], in0=exps[0:ROW_TILES, :], scalar1=inverse[0:ROW_TILES, 0:1]
+        )
         nc.sync.dma_start(
             out=out[0].rearrange("(i p) o -> i (p o)", p=P), in_=weights[0:ROW_TILES, :]
         )

@@ -212,8 +212,9 @@ def tile_parallelcoattention_kernel(tc, embedding, heatm, W_b_words, W_b_scales,
             for i in range(run):
                 nc.tensor.matmul(out=idle_sum[:], lhsT=idle_weights[:], rhs=columns, start=True, stop=True)
 
-        keep_busy(idle_columns[:], 10)
-        interleave(0, 2, 0, nc.scalar.copy)
+        keep_busy(idle_columns[:], 4)
+        interleave(0, 2, 0, nc.vector.tensor_copy)
+        keep_busy(e_grouped[:, 0, 0:P, :].rearrange("p n j -> p (n j)"), 4)
         permute_scales(0)
         permute_scales(1)
         interleave(0, 2, 1, nc.scalar.copy)

@@ -228,36 +228,35 @@ def tile_parallelcoattention_kernel(tc, embedding, heatm, W_b_words, W_b_scales,
         permute_w(1, 1)
         first_product(0, 1)
         first_product(1, 1)
-        interleave(2, 1, 0, nc.vector.tensor_copy)
-        interleave(3, 1, 0, nc.scalar.copy)
-        quantise_e(2, 1, 0)
-        interleave(2, 1, 1, nc.vector.tensor_copy)
-        interleave(3, 1, 1, nc.scalar.copy)
-        quantise_e(2, 1, 1)
-        quantise_e(3, 1, 0)
-        quantise_e(3, 1, 1)
+        for g in range(PASSES):
+            interleave(2, 1, g, nc.vector.tensor_copy)
+            interleave(3, 1, g, nc.scalar.copy)
+        for c in (2, 3):
+            for g in range(PASSES):
+                quantise_e(c, 1, g)
+        for h in range(HALVES):
+            for c in (2, 3):
+                first_product(c, h)
         copy_out(0, 0)
         copy_out(1, 0)
-        first_product(2, 0)
-        first_product(3, 0)
-        first_product(2, 1)
-        first_product(3, 1)
-        interleave(4, 2, 0, nc.vector.tensor_copy)
-        interleave(4, 2, 1, nc.vector.tensor_copy)
+        for g in range(PASSES):
+            for c in (4, 5):
+                interleave(c, 1, g, nc.vector.tensor_copy)
+        for g in range(PASSES):
+            quantise_e(4, 1, g)
         copy_out(0, 1)
         copy_out(1, 1)
-        quantise_e(4, 2, 0)
-        quantise_e(4, 2, 1)
+        for g in range(PASSES):
+            quantise_e(5, 1, g)
+        quantise_next()
+        quantise_next()
         interleave(6, 2, 0, nc.scalar.copy)
         interleave(6, 2, 1, nc.vector.tensor_copy)
-        quantise_next()
-        quantise_next()
         quantise_e(6, 2, 0)
         quantise_e(6, 2, 1)
-        copy_out(2, 0)
-        copy_out(3, 0)
-        copy_out(2, 1)
-        copy_out(3, 1)
+        for h in range(HALVES):
+            for c in (2, 3):
+                copy_out(c, h)
 
         later = [(c, h) for c in range(4, ROW_TILES) for h in range(HALVES)]
         for c, h in later[:LEAD]:

@@ -94,13 +94,13 @@ def tile_parallelcoattention_kernel(tc, embedding, heatm, W_b_words, W_b_scales,
                 in_=W_b_words[g, :, cols, :].rearrange("p n j -> p (n j)").bitcast(I32),
             )
 
-        load_embedding_pass(0, 0)
+        for g in range(PASSES):
+            load_embedding_pass(0, g)
         for quadrant in range(4):
             nc.sync.dma_start(
                 out=ws_raw[32 * quadrant : 32 * quadrant + 4 * PASSES, :].bitcast(I32),
                 in_=W_b_scales[:, 4 * quadrant : 4 * quadrant + 4, :].bitcast(I32),
             )
-        load_embedding_pass(0, 1)
         load_w_pass(0, 0)
         load_w_pass(0, 1)
         load_w_pass(1, 0)
@@ -215,15 +215,15 @@ def tile_parallelcoattention_kernel(tc, embedding, heatm, W_b_words, W_b_scales,
         keep_busy(idle_columns[:], 4)
         interleave(0, 2, 0, nc.vector.tensor_copy)
         keep_busy(e_grouped[:, 0, 0:P, :].rearrange("p n j -> p (n j)"), 4)
-        permute_scales(0)
-        permute_scales(1)
         interleave(0, 2, 1, nc.scalar.copy)
         quantise_e(0, 2, 0)
+        permute_scales(0)
         permute_w(0, 0)
         permute_w(0, 1)
         quantise_e(0, 2, 1)
         first_product(0, 0)
         first_product(1, 0)
+        permute_scales(1)
         permute_w(1, 0)
         permute_w(1, 1)
         first_product(0, 1)

@@ -217,8 +217,8 @@ def tile_parallelcoattention_kernel(tc, embedding, heatm, W_b_words, W_b_scales,
         keep_busy(e_grouped[:, 0, 0:P, :].rearrange("p n j -> p (n j)"), 4)
         interleave(0, 2, 1, nc.scalar.copy)
         quantise_e(0, 2, 0)
-        permute_scales(0)
         permute_w(0, 0)
+        permute_scales(0)
         permute_w(0, 1)
         quantise_e(0, 2, 1)
         first_product(0, 0)

from contextlib import ExitStack

import concourse.mybir as mybir
from concourse.masks import make_identity

F32 = mybir.dt.float32
BF16 = mybir.dt.bfloat16
I32 = mybir.dt.int32
U32 = mybir.dt.uint32
U8 = mybir.dt.uint8
FP8X4 = mybir.dt.float8_e4m3fn_x4
ACT = mybir.ActivationFunctionType
ALU = mybir.AluOpType
AXIS_X = mybir.AxisListType.X

P = 128
PACK = 4
K_PASS = P * PACK
D = 1024
N = 1024
PASSES = D // K_PASS
BANK = 512
HALVES = N // BANK
ROW_TILES = N // P
RUN = 4
CHUNKS = ((0, 2), (2, 2), (4, 2), (6, 2))
PSUM_BANKS = 8
LEAD = 3
LINE = 16

FLOPS = 2 * 2 * N * D * N
BYTES = 2 * D * N + D * D + D * D // 32 + 4 * N


def tile_parallelcoattention_kernel(tc, embedding, heatm, W_b_words, W_b_scales, out):
    nc = tc.nc
    with ExitStack() as ctx:
        ctx.enter_context(tc.manual_schedule())
        keep = ctx.enter_context(tc.tile_pool(name="keep", bufs=1))
        t_pool = ctx.enter_context(tc.tile_pool(name="t_pool", bufs=ROW_TILES))
        banks = ctx.enter_context(tc.psum_pool(name="banks", bufs=PSUM_BANKS))

        e_raw = {
            (q, g): keep.tile([P, PACK, tiles * P], BF16, name="e_raw%d%d" % (q, g))
            for q, (first, tiles) in enumerate(CHUNKS)
            for g in range(PASSES)
        }
        e_grouped = keep.tile([P, PASSES, N, PACK], BF16, align_bytes=256)
        e_codes = keep.tile([P, PASSES, N], U32, align_bytes=256)
        e_scales = keep.tile([P, PASSES, N], U8, align_bytes=256)
        w_raw = [keep.tile([P, PASSES, BANK], I32, name="w_raw%d" % h, align_bytes=256) for h in range(HALVES)]
        w_codes = [
            keep.tile([P, PASSES, PACK, P], I32, name="w_codes%d" % h, align_bytes=256) for h in range(HALVES)
        ]
        ws_raw = keep.tile([P, D], U8, align_bytes=256)
        ws = [keep.tile([P, PACK, P], U8, name="ws%d" % h, align_bytes=256) for h in range(HALVES)]
        ident_f32 = keep.tile([P, P], F32)
        half_max = keep.tile([P, ROW_TILES * HALVES], F32)
        minus_tanh = keep.tile([P, ROW_TILES * HALVES], F32)
        minus_m = keep.tile([P, P], F32)
        tile_sum = keep.tile([P, 1], F32)
        ones = keep.tile([P, P], F32)
        table_warm = keep.tile([P, 1], F32)
        idle_weights = keep.tile([P, P], BF16)
        idle_columns = keep.tile([P, BANK], BF16)

        nc.vector.memset(ws_raw[:].bitcast(I32), 0)
        nc.vector.memset(idle_weights[:], 0.0)
        nc.vector.memset(idle_columns[:], 0.0)
        nc.vector.memset(minus_m[:], 0.0)
        nc.vector.memset(tile_sum[:], 0.0)
        nc.vector.memset(table_warm[:], 0.0)
        nc.vector.memset(ones[:], 1.0)
        nc.scalar.activation(out=table_warm[:], in_=table_warm[:], func=ACT.Tanh)
        make_identity(nc, ident_f32[:])

        def load_w(h):
            cols = slice(h * BANK, (h + 1) * BANK)
            for g in range(PASSES):
                nc.sync.dma_start(
                    out=w_raw[h][:, g, :],
                    in_=W_b_words[g, :, cols, :].rearrange("p n j -> p (n j)").bitcast(I32),
                )

        def load_embedding_pass(q, g):
            first, tiles = CHUNKS[q]
            rows = embedding[0, g * K_PASS : (g + 1) * K_PASS, first * P : (first + tiles) * P]
            nc.sync.dma_start(out=e_raw[q, g][:], in_=rows.rearrange("(p j) n -> p j n", j=PACK))

        def load_w_pass(h, g):
            cols = slice(h * BANK, (h + 1) * BANK)
            nc.sync.dma_start(
                out=w_raw[h][:, g, :],
                in_=W_b_words[g, :, cols, :].rearrange("p n j -> p (n j)").bitcast(I32),
            )

        for g in range(PASSES):
            load_embedding_pass(0, g)
        for quadrant in range(4):
            nc.sync.dma_start(
                out=ws_raw[32 * quadrant : 32 * quadrant + 4 * PASSES, :].bitcast(I32),
                in_=W_b_scales[:, 4 * quadrant : 4 * quadrant + 4, :].bitcast(I32),
            )
        load_w_pass(0, 0)
        load_w_pass(0, 1)
        load_w_pass(1, 0)
        load_w_pass(1, 1)
        load_embedding_pass(1, 0)
        load_embedding_pass(1, 1)
        load_embedding_pass(2, 0)
        load_embedding_pass(2, 1)
        load_embedding_pass(3, 0)
        load_embedding_pass(3, 1)

        def interleave(first, tiles, g, copy):
            q = max(i for i, (start, count) in enumerate(CHUNKS) if start <= first)
            cols = slice(first * P, (first + tiles) * P)
            local = slice((first - CHUNKS[q][0]) * P, (first + tiles - CHUNKS[q][0]) * P)
            copy(
                out=e_grouped[:, g, cols, :].rearrange("p (c i) j -> p c j i", i=RUN),
                in_=e_raw[q, g][:, :, local].rearrange("p j (c i) -> p c j i", i=RUN),
            )

        def quantise_e(first, tiles, g):
            cols = slice(first * P, (first + tiles) * P)
            nc.vector.quantize_mx(
                out=e_codes[:, g, cols].bitcast(FP8X4),
                scales=e_scales[:, g, cols],
                in_=e_grouped[:, g, cols, :].rearrange("p n j -> p (n j)"),
            )

        def permute_w(h, g):
            nc.vector.tensor_copy(
                out=w_codes[h][:, g, :, :].rearrange("p j (c i) -> p c j i", i=LINE // 4),
                in_=w_raw[h][:, g, :].rearrange("p (c i j) -> p c j i", i=LINE // 4, j=PACK),
            )

        def permute_scales(h):
            nc.vector.tensor_copy(
                out=ws[h][:].rearrange("p j (c i) -> p c j i", i=LINE),
                in_=ws_raw[:, h * BANK : (h + 1) * BANK].rearrange("p (c i j) -> p c j i", i=LINE, j=PACK),
            )

        t_sum = {}
        t_grouped = {}
        t_codes = {}
        t_scales = {}
        copied = []

        def first_product(c, h):
            rows = slice(c * P, (c + 1) * P)
            t_sum[c, h] = banks.tile([P, PACK, P], F32, name="t_sum", tag="bank")
            for j in range(PACK):
                for g in range(PASSES):
                    nc.tensor.matmul_mx(
                        out=t_sum[c, h][:, j, :],
                        lhsT=w_codes[h][:, g, j, :].bitcast(FP8X4),
                        lhsT_scale=ws[h][4 * g : P, j, :],
                        rhs=e_codes[:, g, rows].bitcast(FP8X4),
                        rhs_scale=e_scales[:, g, rows],
                        start=(g == 0),
                        stop=(g == PASSES - 1),
                    )

        def copy_out(c, h):
            if h == 0:
                t_grouped[c] = t_pool.tile(
                    [P, HALVES, P, PACK], BF16, name="t_grouped", align_bytes=256
                )
            nc.scalar.copy(
                out=t_grouped[c][:, h, :, :], in_=t_sum[c, h][:].rearrange("p j n -> p n j")
            )
            if h == HALVES - 1:
                copied.append(c)

        def quantise_t(c):
            t_codes[c] = t_pool.tile([P, HALVES, P], U32, name="t_codes", align_bytes=256)
            t_scales[c] = t_pool.tile([P, HALVES, P], U8, name="t_scales", align_bytes=256)
            nc.vector.quantize_mx(
                out=t_codes[c][:].rearrange("p g n -> p (g n)").bitcast(FP8X4),
                scales=t_scales[c][:].rearrange("p g n -> p (g n)"),
                in_=t_grouped[c][:].rearrange("p g n j -> p (g n j)"),
            )

        def quantise_next():
            if copied:
                quantise_t(copied[0])
                copied.remove(copied[0])

        def second_product(c):
            for half in range(HALVES):
                cols = slice(half * BANK, (half + 1) * BANK)
                c_sum = banks.tile([P, BANK], F32, name="c_sum", tag="bank")
                for g2 in range(PASSES):
                    nc.tensor.matmul_mx(
                        out=c_sum[:],
                        lhsT=t_codes[c][:, g2, :].bitcast(FP8X4),
                        lhsT_scale=t_scales[c][:, g2, :],
                        rhs=e_codes[:, g2, cols].bitcast(FP8X4),
                        rhs_scale=e_scales[:, g2, cols],
                        start=(g2 == 0),
                        stop=(g2 == PASSES - 1),
                    )
                place = c * HALVES + half
                nc.vector.tensor_reduce(
                    out=half_max[:, place : place + 1], in_=c_sum[:], axis=AXIS_X, op=ALU.max
                )

        idle_sum = banks.tile([P, BANK], F32, name="idle_sum", tag="bank")

        def keep_busy(columns, run):
            for i in range(run):
                nc.tensor.matmul(out=idle_sum[:], lhsT=idle_weights[:], rhs=columns, start=True, stop=True)

        keep_busy(idle_columns[:], 4)
        interleave(0, 2, 0, nc.vector.tensor_copy)
        keep_busy(e_grouped[:, 0, 0:P, :].rearrange("p n j -> p (n j)"), 4)
        interleave(0, 2, 1, nc.scalar.copy)
        quantise_e(0, 2, 0)
        permute_w(0, 0)
        permute_scales(0)
        permute_w(0, 1)
        quantise_e(0, 2, 1)
        first_product(0, 0)
        first_product(1, 0)
        permute_scales(1)
        permute_w(1, 0)
        permute_w(1, 1)
        first_product(0, 1)
        first_product(1, 1)
        for g in range(PASSES):
            interleave(2, 1, g, nc.vector.tensor_copy)
            interleave(3, 1, g, nc.scalar.copy)
        for c in (2, 3):
            for g in range(PASSES):
                quantise_e(c, 1, g)
        for h in range(HALVES):
            for c in (2, 3):
                first_product(c, h)
        copy_out(0, 0)
        copy_out(1, 0)
        for g in range(PASSES):
            for c in (4, 5):
                interleave(c, 1, g, nc.vector.tensor_copy)
        for g in range(PASSES):
            quantise_e(4, 1, g)
        copy_out(0, 1)
        copy_out(1, 1)
        for g in range(PASSES):
            quantise_e(5, 1, g)
        quantise_next()
        quantise_next()
        interleave(6, 2, 0, nc.scalar.copy)
        interleave(6, 2, 1, nc.vector.tensor_copy)
        quantise_e(6, 2, 0)
        quantise_e(6, 2, 1)
        for h in range(HALVES):
            for c in (2, 3):
                copy_out(c, h)

        later = [(c, h) for c in range(4, ROW_TILES) for h in range(HALVES)]
        for c, h in later[:LEAD]:
            first_product(c, h)
            copy_out(c, h)
        for c in range(ROW_TILES):
            while c not in t_codes:
                quantise_next()
            second_product(c)
            quantise_next()
            for c1, h1 in later[LEAD + c : LEAD + c + 1]:
                first_product(c1, h1)
                copy_out(c1, h1)

        last = ROW_TILES * HALVES - 1
        nc.scalar.activation(out=minus_tanh[:, 0:last], in_=half_max[:, 0:last], func=ACT.Tanh, scale=-1.0)
        nc.scalar.activation(
            out=minus_tanh[:, last : last + 1], in_=half_max[:, last : last + 1], func=ACT.Tanh, scale=-1.0
        )
        earlier_min = keep.tile([P, 1], F32)
        nc.vector.tensor_reduce(out=earlier_min[:], in_=minus_tanh[:, 0:last], axis=AXIS_X, op=ALU.min)
        spread = banks.tile([P, 2, P], F32, name="spread", tag="bank")
        nc.tensor.transpose(spread[:, 0, :], earlier_min[:, 0:1].to_broadcast([P, P]), ident_f32[:])
        nc.tensor.transpose(
            spread[:, 1, :], minus_tanh[:, last : last + 1].to_broadcast([P, P]), ident_f32[:]
        )
        nc.vector.tensor_reduce(
            out=minus_m[:, 0:ROW_TILES],
            in_=minus_tanh[:].rearrange("p (i h) -> p i h", h=HALVES),
            axis=AXIS_X,
            op=ALU.min,
        )
        minus_m_turned = banks.tile([P, P], F32, name="minus_m_turned", tag="bank")
        nc.tensor.transpose(minus_m_turned[:], minus_m[:], ident_f32[:])
        minus_top = keep.tile([P, 1], F32)
        nc.vector.tensor_reduce(
            out=minus_top[:], in_=spread[:].rearrange("p a n -> p (a n)"), axis=AXIS_X, op=ALU.min
        )
        exps = keep.tile([P, P], F32)
        nc.scalar.activation(
            out=exps[0:ROW_TILES, :],
            in_=minus_m_turned[0:ROW_TILES, :],
            func=ACT.Exp,
            scale=-1.0,
            bias=minus_top[0:ROW_TILES, 0:1],
            accum_out=tile_sum[0:ROW_TILES, :],
        )
        total = banks.tile([P, 1], F32, name="total", tag="bank")
        nc.tensor.matmul(out=total[:], lhsT=ones[:], rhs=tile_sum[:], start=True, stop=True)
        inverse = keep.tile([P, 1], F32)
        nc.vector.reciprocal(out=inverse[0:ROW_TILES, :], in_=total[0:ROW_TILES, :])
        weights = keep.tile([P, P], F32)
        nc.vector.tensor_scalar_mul(
            out=weights[0:ROW_TILES, :], in0=exps[0:ROW_TILES, :], scalar1=inverse[0:ROW_TILES, 0:1]
        )
        nc.sync.dma_start(
            out=out[0].rearrange("(i p) o -> i (p o)", p=P), in_=weights[0:ROW_TILES, :]
        )
